import numpy as np
import ml_dtypes


def mxq(x, axis, fmt="e4m3"):
    dtype, down = {"e4m3": (ml_dtypes.float8_e4m3fn, 7), "e5m2": (ml_dtypes.float8_e5m2, 14)}[fmt]
    v = np.moveaxis(np.asarray(x, np.float32).astype(ml_dtypes.bfloat16).astype(np.float64), axis, -1)
    blocks = v.reshape(v.shape[:-1] + (-1, 32))
    amax = np.abs(blocks).max(-1, keepdims=True)
    byte = np.maximum(np.where(amax > 0, np.frexp(amax)[1] - 1 + 127, 0) - down, 1)
    scale = np.exp2(byte - 127.0)
    codes = (blocks / scale).astype(np.float32).astype(dtype).astype(np.float64)
    return np.moveaxis((codes * scale).reshape(v.shape), -1, axis)


WIDE = False


def mx_kscale(k):
    if not WIDE:
        return np.ones(k)
    levels = np.array([10, -10, 5, -5, 0])
    a = np.random.permutation(np.resize(levels, k // 512 * 4)).reshape(k // 512, 4)
    idx = np.arange(k)
    return np.exp2(a[idx // 512, idx % 128 // 32])


BF16 = ml_dtypes.bfloat16


def bf(x):
    return np.asarray(x, np.float32).astype(BF16)


def f64(x):
    return np.asarray(x).astype(np.float64)


B, S, D_IN, D_MODEL = 8, 512, 1024, 512


def relu(v):
    return np.maximum(v, 0.0)


def setup_inputs():
    s = mx_kscale(D_MODEL)
    t = mx_kscale(S)
    return {"qp": bf(np.random.standard_normal((B, S, D_MODEL)) * 0.4 * s),
            "kp": bf(np.random.standard_normal((B, S, D_MODEL)) * 0.4 / s * t[:, None]),
            "vp": bf(np.random.standard_normal((B, S, D_MODEL)) * 0.25 / t[:, None]),
            "mask": bf(np.random.standard_normal((1, S, S)) * 0.1 * t)}


def reference(qp, kp, vp, mask):
    scores = relu(mxq(f64(qp), 2, "e4m3") @ mxq(f64(kp), 2, "e4m3").transpose(0, 2, 1))
    logits = scores / np.sqrt(D_MODEL) + f64(mask)
    return relu(mxq(logits, 2, "e4m3") @ mxq(f64(vp), 1, "e4m3"))

@@ -1,0 +1,196 @@
+import math
+from contextlib import ExitStack
+
+import concourse.mybir as mybir
+from concourse.masks import make_identity
+
+F32 = mybir.dt.float32
+BF16 = mybir.dt.bfloat16
+U32 = mybir.dt.uint32
+U8 = mybir.dt.uint8
+FP8X4 = mybir.dt.float8_e4m3fn_x4
+ALU = mybir.AluOpType
+ACT = mybir.ActivationFunctionType
+
+NB = 8
+S = 512
+D = 512
+P = 128
+FLOPS = 2 * 2 * NB * S * S * D
+
+INV_SQRT_D = 1.0 / math.sqrt(D)
+PRE = 3
+COPY_ENGINE = ("s", "s", "s", "s")
+OUT_ENGINE = ("s", "s", "s", "s")
+LOGIT_FORM = ("s", "s", "v", "v")
+MANUAL = False
+
+
+def tile_scaledconvolutionaldotproduct_pa_t_kernel(tc, qp, kp, vp, mask, out):
+    nc = tc.nc
+    with ExitStack() as ctx:
+        if MANUAL:
+            ctx.enter_context(tc.manual_schedule())
+        const = ctx.enter_context(tc.tile_pool(name="const", bufs=1))
+        raw = ctx.enter_context(tc.tile_pool(name="raw", bufs=PRE + 1))
+        work = ctx.enter_context(tc.tile_pool(name="work", bufs=2))
+        keep = ctx.enter_context(tc.tile_pool(name="keep", bufs=3))
+        ps_t = ctx.enter_context(tc.psum_pool(name="ps_t", bufs=3))
+        ps_1 = ctx.enter_context(tc.psum_pool(name="ps_1", bufs=3))
+        ps_2 = ctx.enter_context(tc.psum_pool(name="ps_2", bufs=2))
+
+        ident = const.tile([P, P], F32)
+        make_identity(nc, ident[:])
+        m_sb = const.tile([P, 4 * S], BF16)
+        mask_g = const.tile([P, 4 * S], BF16, align_bytes=64)
+
+        state = {}
+
+        def copy_out(engine, dst, src):
+            if engine == "s":
+                nc.scalar.copy(out=dst, in_=src)
+            else:
+                nc.vector.tensor_copy(out=dst, in_=src)
+
+        def load(b):
+            q_sb = raw.tile([P, 4 * D], BF16)
+            k_sb = raw.tile([P, 4 * D], BF16)
+            v_sb = raw.tile([P, 4 * D], BF16)
+            nc.sync.dma_start(out=q_sb[:], in_=qp[b].rearrange("(p j) d -> p (j d)", j=4))
+            nc.sync.dma_start(out=k_sb[:], in_=kp[b].rearrange("(p j) d -> p (j d)", j=4))
+            if b == 0:
+                nc.sync.dma_start(out=m_sb[:], in_=mask[0].rearrange("(p j) d -> p (j d)", j=4))
+            nc.sync.dma_start(out=v_sb[:], in_=vp[b].rearrange("(p j) d -> p (j d)", j=4))
+            state[("raw", b)] = (q_sb, k_sb, v_sb)
+
+        def prepare_mask():
+            m32 = m_sb[:].bitcast(F32).rearrange("r (j p u) -> r j p u", j=4, u=2)
+            g32 = mask_g[:].bitcast(F32)
+            for h in range(2):
+                tp = ps_t.tile([P, 2, 2, P], F32, tag="tp")
+                for jj in range(2):
+                    for u in range(2):
+                        nc.tensor.transpose(tp[:, jj, u, :], m32[:, 2 * h + jj, :, u], ident[:])
+                nc.vector.tensor_copy(
+                    out=g32[:, 512 * h : 512 * (h + 1)].rearrange("p (j r u) -> p j r u", j=2, u=2),
+                    in_=tp[:].rearrange("p j u r -> p j r u"),
+                )
+
+        def front(b):
+            q_sb, k_sb, v_sb = state[("raw", b)]
+            qk_g = work.tile([P, 8 * S], BF16, align_bytes=64)
+            g32 = qk_g[:].bitcast(F32)
+            n = 0
+            for src in (k_sb, q_sb):
+                s32 = src[:].bitcast(F32)
+                base = 1024 if src is k_sb else 0
+                for h in range(2):
+                    tp = ps_t.tile([P, 2, 2, P], F32, tag="tp")
+                    for jj in range(2):
+                        for u in range(2):
+                            c0 = (2 * h + jj) * 256 + u * 128
+                            nc.tensor.transpose(tp[:, jj, u, :], s32[:, c0 : c0 + 128], ident[:])
+                    copy_out(
+                        COPY_ENGINE[n],
+                        g32[:, base + 512 * h : base + 512 * (h + 1)].rearrange(
+                            "p (j r u) -> p j r u", j=2, u=2
+                        ),
+                        tp[:].rearrange("p j u r -> p j r u"),
+                    )
+                    n += 1
+            v_g = work.tile([P, 4 * D], BF16, align_bytes=64)
+            nc.vector.tensor_copy(
+                out=v_g[:].rearrange("p (c i t) -> p c t i", i=4, t=4),
+                in_=v_sb[:].rearrange("p (t c i) -> p c t i", i=4, t=4),
+            )
+            qk_c = keep.tile([P, 2 * S], U32, align_bytes=64)
+            qk_s = keep.tile([P, 2 * S], U8, align_bytes=64)
+            nc.vector.quantize_mx(out=qk_c[:].bitcast(FP8X4), scales=qk_s[:], in_=qk_g[:])
+            v_c = keep.tile([P, D], U32, align_bytes=64, bufs=4)
+            v_s = keep.tile([P, D], U8, align_bytes=64, bufs=4)
+            nc.vector.quantize_mx(out=v_c[:].bitcast(FP8X4), scales=v_s[:], in_=v_g[:])
+            state[("qk", b)] = (qk_c, qk_s)
+            state[("v", b)] = (v_c, v_s)
+
+        def mid(b):
+            qk_c, qk_s = state[("qk", b)]
+            l_g = work.tile([P, 4 * S], BF16, align_bytes=64)
+            x_g = work.tile([P, 4 * S], BF16, align_bytes=64)
+            for j in range(4):
+                s1 = ps_1.tile([P, 4, P], F32, tag="s1")
+                for t in range(4):
+                    kc = slice(S + P * t, S + P * (t + 1))
+                    qc = slice(P * j, P * (j + 1))
+                    nc.tensor.matmul_mx(
+                        out=s1[:, t, :],
+                        lhsT=qk_c[:, kc].bitcast(FP8X4),
+                        lhsT_scale=qk_s[:, kc],
+                        rhs=qk_c[:, qc].bitcast(FP8X4),
+                        rhs_scale=qk_s[:, qc],
+                        start=True,
+                        stop=True,
+                    )
+                cols = slice(4 * P * j, 4 * P * (j + 1))
+                s1_rt = s1[:].rearrange("p t r -> p r t")
+                if LOGIT_FORM[j] == "s":
+                    a = work.tile([P, P, 4], F32, bufs=3)
+                    nc.scalar.activation(out=a[:], in_=s1_rt, func=ACT.Relu, scale=INV_SQRT_D)
+                    nc.vector.tensor_tensor(
+                        out=l_g[:, cols],
+                        in0=a[:].rearrange("p r t -> p (r t)"),
+                        in1=mask_g[:, cols],
+                        op=ALU.add,
+                    )
+                else:
+                    nc.vector.scalar_tensor_tensor(
+                        out=x_g[:, cols].rearrange("p (r t) -> p r t", t=4),
+                        in0=s1_rt,
+                        scalar=INV_SQRT_D,
+                        in1=mask_g[:, cols].rearrange("p (r t) -> p r t", t=4),
+                        op0=ALU.mult,
+                        op1=ALU.add,
+                    )
+                    nc.vector.tensor_tensor(
+                        out=l_g[:, cols], in0=x_g[:, cols], in1=mask_g[:, cols], op=ALU.max
+                    )
+            l_c = keep.tile([P, S], U32, align_bytes=64)
+            l_s = keep.tile([P, S], U8, align_bytes=64)
+            nc.vector.quantize_mx(out=l_c[:].bitcast(FP8X4), scales=l_s[:], in_=l_g[:])
+            state[("l", b)] = (l_c, l_s)
+
+        def back(b):
+            l_c, l_s = state[("l", b)]
+            v_c, v_s = state[("v", b)]
+            o_sb = keep.tile([P, 4 * D], F32)
+            for j in range(4):
+                s2 = ps_2.tile([P, D], F32, tag="s2")
+                qc = slice(P * j, P * (j + 1))
+                nc.tensor.matmul_mx(
+                    out=s2[:],
+                    lhsT=l_c[:, qc].bitcast(FP8X4),
+                    lhsT_scale=l_s[:, qc],
+                    rhs=v_c[:].bitcast(FP8X4),
+                    rhs_scale=v_s[:],
+                    start=True,
+                    stop=True,
+                )
+                dst = o_sb[:, D * j : D * (j + 1)]
+                if OUT_ENGINE[j] == "s":
+                    nc.scalar.activation(out=dst, in_=s2[:], func=ACT.Relu)
+                else:
+                    nc.vector.tensor_scalar_max(out=dst, in0=s2[:], scalar1=0.0)
+            nc.sync.dma_start(out=out[b].rearrange("(p j) f -> p (j f)", j=4), in_=o_sb[:])
+
+        for b in range(PRE):
+            load(b)
+        for i in range(NB + 2):
+            if i + PRE < NB:
+                load(i + PRE)
+            if i < NB:
+                front(i)
+            if i == 0:
+                prepare_mask()
+            if 0 <= i - 1 < NB:
+                mid(i - 1)
+            if 0 <= i - 2 < NB:
+                back(i - 2)

@@ -19,11 +19,8 @@ P = 128
 FLOPS = 2 * 2 * NB * S * S * D
 
 INV_SQRT_D = 1.0 / math.sqrt(D)
-PRE = 3
-COPY_ENGINE = ("s", "s", "s", "s")
-OUT_ENGINE = ("s", "s", "s", "s")
-LOGIT_FORM = ("s", "s", "v", "v")
-MANUAL = False
+R_VECTOR_GROUPS = 56
+MANUAL = True
 
 
 def tile_scaledconvolutionaldotproduct_pa_t_kernel(tc, qp, kp, vp, mask, out):
@@ -32,11 +29,10 @@ def tile_scaledconvolutionaldotproduct_pa_t_kernel(tc, qp, kp, vp, mask, out):
         if MANUAL:
             ctx.enter_context(tc.manual_schedule())
         const = ctx.enter_context(tc.tile_pool(name="const", bufs=1))
-        raw = ctx.enter_context(tc.tile_pool(name="raw", bufs=PRE + 1))
+        raw = ctx.enter_context(tc.tile_pool(name="raw", bufs=NB))
         work = ctx.enter_context(tc.tile_pool(name="work", bufs=2))
-        keep = ctx.enter_context(tc.tile_pool(name="keep", bufs=3))
-        ps_t = ctx.enter_context(tc.psum_pool(name="ps_t", bufs=3))
-        ps_1 = ctx.enter_context(tc.psum_pool(name="ps_1", bufs=3))
+        ps_t = ctx.enter_context(tc.psum_pool(name="ps_t", bufs=4))
+        ps_1 = ctx.enter_context(tc.psum_pool(name="ps_1", bufs=2))
         ps_2 = ctx.enter_context(tc.psum_pool(name="ps_2", bufs=2))
 
         ident = const.tile([P, P], F32)
@@ -44,7 +40,29 @@ def tile_scaledconvolutionaldotproduct_pa_t_kernel(tc, qp, kp, vp, mask, out):
         m_sb = const.tile([P, 4 * S], BF16)
         mask_g = const.tile([P, 4 * S], BF16, align_bytes=64)
 
-        state = {}
+        st = {}
+
+        def live(b):
+            return 0 <= b < NB
+
+        def rows(x):
+            return x.rearrange("(p j) d -> p (j d)", j=4)
+
+        def load(b):
+            k_sb = raw.tile([P, 4 * D], BF16)
+            q_sb = raw.tile([P, 4 * D], BF16)
+            v_sb = raw.tile([P, 4 * D], BF16)
+            if b == 0:
+                for x_sb, x in ((k_sb, kp), (q_sb, qp)):
+                    for h in range(2):
+                        half = slice(2 * D * h, 2 * D * (h + 1))
+                        nc.sync.dma_start(out=x_sb[:, half], in_=rows(x[b])[:, half])
+                nc.sync.dma_start(out=m_sb[:], in_=rows(mask[0]))
+            else:
+                nc.sync.dma_start(out=k_sb[:], in_=rows(kp[b]))
+                nc.sync.dma_start(out=q_sb[:], in_=rows(qp[b]))
+            nc.sync.dma_start(out=v_sb[:], in_=rows(vp[b]))
+            st[("raw", b)] = (k_sb, q_sb, v_sb)
 
         def copy_out(engine, dst, src):
             if engine == "s":
@@ -52,145 +70,225 @@ def tile_scaledconvolutionaldotproduct_pa_t_kernel(tc, qp, kp, vp, mask, out):
             else:
                 nc.vector.tensor_copy(out=dst, in_=src)
 
-        def load(b):
-            q_sb = raw.tile([P, 4 * D], BF16)
-            k_sb = raw.tile([P, 4 * D], BF16)
-            v_sb = raw.tile([P, 4 * D], BF16)
-            nc.sync.dma_start(out=q_sb[:], in_=qp[b].rearrange("(p j) d -> p (j d)", j=4))
-            nc.sync.dma_start(out=k_sb[:], in_=kp[b].rearrange("(p j) d -> p (j d)", j=4))
-            if b == 0:
-                nc.sync.dma_start(out=m_sb[:], in_=mask[0].rearrange("(p j) d -> p (j d)", j=4))
-            nc.sync.dma_start(out=v_sb[:], in_=vp[b].rearrange("(p j) d -> p (j d)", j=4))
-            state[("raw", b)] = (q_sb, k_sb, v_sb)
+        def unpack(engine, g32, n, tp):
+            copy_out(
+                engine,
+                g32[:, 512 * n : 512 * (n + 1)].rearrange("p (j r u) -> p j r u", j=2, u=2),
+                tp[:].rearrange("p j u r -> p j r u"),
+            )
 
         def prepare_mask():
             m32 = m_sb[:].bitcast(F32).rearrange("r (j p u) -> r j p u", j=4, u=2)
             g32 = mask_g[:].bitcast(F32)
             for h in range(2):
-                tp = ps_t.tile([P, 2, 2, P], F32, tag="tp")
+                tp = ps_2.tile([P, 2, 2, P], F32, tag="s2")
                 for jj in range(2):
                     for u in range(2):
                         nc.tensor.transpose(tp[:, jj, u, :], m32[:, 2 * h + jj, :, u], ident[:])
-                nc.vector.tensor_copy(
-                    out=g32[:, 512 * h : 512 * (h + 1)].rearrange("p (j r u) -> p j r u", j=2, u=2),
-                    in_=tp[:].rearrange("p j u r -> p j r u"),
-                )
+                unpack("s", g32, h, tp)
 
-        def front(b):
-            q_sb, k_sb, v_sb = state[("raw", b)]
-            qk_g = work.tile([P, 8 * S], BF16, align_bytes=64)
-            g32 = qk_g[:].bitcast(F32)
-            n = 0
+        def transposes(b):
+            if not live(b):
+                return
+            k_sb, q_sb, v_sb = st[("raw", b)]
+            banks = []
             for src in (k_sb, q_sb):
                 s32 = src[:].bitcast(F32)
-                base = 1024 if src is k_sb else 0
                 for h in range(2):
                     tp = ps_t.tile([P, 2, 2, P], F32, tag="tp")
                     for jj in range(2):
                         for u in range(2):
                             c0 = (2 * h + jj) * 256 + u * 128
                             nc.tensor.transpose(tp[:, jj, u, :], s32[:, c0 : c0 + 128], ident[:])
-                    copy_out(
-                        COPY_ENGINE[n],
-                        g32[:, base + 512 * h : base + 512 * (h + 1)].rearrange(
-                            "p (j r u) -> p j r u", j=2, u=2
-                        ),
-                        tp[:].rearrange("p j u r -> p j r u"),
-                    )
-                    n += 1
-            v_g = work.tile([P, 4 * D], BF16, align_bytes=64)
-            nc.vector.tensor_copy(
-                out=v_g[:].rearrange("p (c i t) -> p c t i", i=4, t=4),
-                in_=v_sb[:].rearrange("p (t c i) -> p c t i", i=4, t=4),
+                    banks.append(tp)
+            st[("tp", b)] = banks
+            qk_g = work.tile([P, 8 * S], BF16, align_bytes=64)
+            qk_c = work.tile([P, 2 * S], U32, align_bytes=64)
+            qk_s = work.tile([P, 2 * S], U8, align_bytes=64)
+            st[("qk", b)] = (qk_g, qk_c, qk_s)
+
+        def copies(b, engines):
+            if not live(b):
+                return
+            g32 = st[("qk", b)][0][:].bitcast(F32)
+            for n in range(4):
+                unpack(engines[n], g32, n, st[("tp", b)][n])
+
+        def quantise_qk(b, part):
+            if not live(b):
+                return
+            qk_g, qk_c, qk_s = st[("qk", b)]
+            w = slice(S * part, S * (part + 1))
+            nc.vector.quantize_mx(
+                out=qk_c[:, w].bitcast(FP8X4),
+                scales=qk_s[:, w],
+                in_=qk_g[:, 4 * S * part : 4 * S * (part + 1)],
             )
-            qk_c = keep.tile([P, 2 * S], U32, align_bytes=64)
-            qk_s = keep.tile([P, 2 * S], U8, align_bytes=64)
-            nc.vector.quantize_mx(out=qk_c[:].bitcast(FP8X4), scales=qk_s[:], in_=qk_g[:])
-            v_c = keep.tile([P, D], U32, align_bytes=64, bufs=4)
-            v_s = keep.tile([P, D], U8, align_bytes=64, bufs=4)
-            nc.vector.quantize_mx(out=v_c[:].bitcast(FP8X4), scales=v_s[:], in_=v_g[:])
-            state[("qk", b)] = (qk_c, qk_s)
-            state[("v", b)] = (v_c, v_s)
 
-        def mid(b):
-            qk_c, qk_s = state[("qk", b)]
-            l_g = work.tile([P, 4 * S], BF16, align_bytes=64)
-            x_g = work.tile([P, 4 * S], BF16, align_bytes=64)
-            for j in range(4):
-                s1 = ps_1.tile([P, 4, P], F32, tag="s1")
-                for t in range(4):
-                    kc = slice(S + P * t, S + P * (t + 1))
-                    qc = slice(P * j, P * (j + 1))
-                    nc.tensor.matmul_mx(
-                        out=s1[:, t, :],
-                        lhsT=qk_c[:, kc].bitcast(FP8X4),
-                        lhsT_scale=qk_s[:, kc],
-                        rhs=qk_c[:, qc].bitcast(FP8X4),
-                        rhs_scale=qk_s[:, qc],
-                        start=True,
-                        stop=True,
-                    )
-                cols = slice(4 * P * j, 4 * P * (j + 1))
-                s1_rt = s1[:].rearrange("p t r -> p r t")
-                if LOGIT_FORM[j] == "s":
-                    a = work.tile([P, P, 4], F32, bufs=3)
-                    nc.scalar.activation(out=a[:], in_=s1_rt, func=ACT.Relu, scale=INV_SQRT_D)
-                    nc.vector.tensor_tensor(
-                        out=l_g[:, cols],
-                        in0=a[:].rearrange("p r t -> p (r t)"),
-                        in1=mask_g[:, cols],
-                        op=ALU.add,
-                    )
-                else:
-                    nc.vector.scalar_tensor_tensor(
-                        out=x_g[:, cols].rearrange("p (r t) -> p r t", t=4),
-                        in0=s1_rt,
-                        scalar=INV_SQRT_D,
-                        in1=mask_g[:, cols].rearrange("p (r t) -> p r t", t=4),
-                        op0=ALU.mult,
-                        op1=ALU.add,
-                    )
-                    nc.vector.tensor_tensor(
-                        out=l_g[:, cols], in0=x_g[:, cols], in1=mask_g[:, cols], op=ALU.max
-                    )
-            l_c = keep.tile([P, S], U32, align_bytes=64)
-            l_s = keep.tile([P, S], U8, align_bytes=64)
-            nc.vector.quantize_mx(out=l_c[:].bitcast(FP8X4), scales=l_s[:], in_=l_g[:])
-            state[("l", b)] = (l_c, l_s)
-
-        def back(b):
-            l_c, l_s = state[("l", b)]
-            v_c, v_s = state[("v", b)]
-            o_sb = keep.tile([P, 4 * D], F32)
-            for j in range(4):
-                s2 = ps_2.tile([P, D], F32, tag="s2")
-                qc = slice(P * j, P * (j + 1))
+        def scores(b, j):
+            if not live(b):
+                return
+            qk_g, qk_c, qk_s = st[("qk", b)]
+            s1 = ps_1.tile([P, 4, P], F32, tag="s1")
+            for t in range(4):
+                kc = slice(P * t, P * (t + 1))
+                qc = slice(S + P * j, S + P * (j + 1))
                 nc.tensor.matmul_mx(
-                    out=s2[:],
-                    lhsT=l_c[:, qc].bitcast(FP8X4),
-                    lhsT_scale=l_s[:, qc],
-                    rhs=v_c[:].bitcast(FP8X4),
-                    rhs_scale=v_s[:],
+                    out=s1[:, t, :],
+                    lhsT=qk_c[:, kc].bitcast(FP8X4),
+                    lhsT_scale=qk_s[:, kc],
+                    rhs=qk_c[:, qc].bitcast(FP8X4),
+                    rhs_scale=qk_s[:, qc],
                     start=True,
                     stop=True,
                 )
-                dst = o_sb[:, D * j : D * (j + 1)]
-                if OUT_ENGINE[j] == "s":
-                    nc.scalar.activation(out=dst, in_=s2[:], func=ACT.Relu)
-                else:
-                    nc.vector.tensor_scalar_max(out=dst, in0=s2[:], scalar1=0.0)
-            nc.sync.dma_start(out=out[b].rearrange("(p j) f -> p (j f)", j=4), in_=o_sb[:])
+            st[("s1", b, j)] = s1
 
-        for b in range(PRE):
+        def logits(b, j):
+            if not live(b):
+                return
+            if j == 0:
+                x_g = work.tile([P, 4 * S], BF16, align_bytes=64)
+                st[("x", b)] = x_g
+            x_g = st[("x", b)]
+            cols = slice(4 * P * j, 4 * P * (j + 1))
+            nc.vector.scalar_tensor_tensor(
+                out=x_g[:, cols].rearrange("p (r t) -> p r t", t=4),
+                in0=st[("s1", b, j)][:].rearrange("p t r -> p r t"),
+                scalar=INV_SQRT_D,
+                in1=mask_g[:, cols].rearrange("p (r t) -> p r t", t=4),
+                op0=ALU.mult,
+                op1=ALU.add,
+            )
+
+        def clamp(b):
+            if not live(b):
+                return
+            l_g = work.tile([P, 4 * S], BF16, align_bytes=64)
+            nc.vector.tensor_tensor(out=l_g[:], in0=st[("x", b)][:], in1=mask_g[:], op=ALU.max)
+            st[("l", b)] = l_g
+
+        def quantise_l(b):
+            if not live(b):
+                return
+            l_c = work.tile([P, S], U32, align_bytes=64)
+            l_s = work.tile([P, S], U8, align_bytes=64)
+            nc.vector.quantize_mx(out=l_c[:].bitcast(FP8X4), scales=l_s[:], in_=st[("l", b)][:])
+            st[("lc", b)] = (l_c, l_s)
+
+        def regroup(b, engine, lo, hi):
+            if not live(b) or lo == hi:
+                return
+            if ("vg", b) not in st:
+                v_g = work.tile([P, 4 * D], BF16, align_bytes=64)
+                st[("vg", b)] = v_g
+            copy_out(
+                engine,
+                st[("vg", b)][:].rearrange("p (c i t) -> p c t i", i=4, t=4)[:, lo:hi],
+                st[("raw", b)][2][:].rearrange("p (t c i) -> p c t i", i=4, t=4)[:, lo:hi],
+            )
+
+        def quantise_v(b):
+            if not live(b):
+                return
+            v_c = work.tile([P, D], U32, align_bytes=64)
+            v_s = work.tile([P, D], U8, align_bytes=64)
+            nc.vector.quantize_mx(out=v_c[:].bitcast(FP8X4), scales=v_s[:], in_=st[("vg", b)][:])
+            st[("vc", b)] = (v_c, v_s)
+
+        def product(b, j, spare=False):
+            if not live(b):
+                return
+            l_c, l_s = st[("lc", b)]
+            v_c, v_s = st[("vc", b)]
+            if spare:
+                s2 = ps_t.tile([P, D], F32, tag="tp")
+            else:
+                s2 = ps_2.tile([P, D], F32, tag="s2")
+            qc = slice(P * j, P * (j + 1))
+            nc.tensor.matmul_mx(
+                out=s2[:],
+                lhsT=l_c[:, qc].bitcast(FP8X4),
+                lhsT_scale=l_s[:, qc],
+                rhs=v_c[:].bitcast(FP8X4),
+                rhs_scale=v_s[:],
+                start=True,
+                stop=True,
+            )
+            st[("s2", b, j)] = s2
+
+        def result(b, j, engine):
+            if not live(b):
+                return
+            if j == 0:
+                o_sb = work.tile([P, 4 * D], F32, bufs=3)
+                st[("o", b)] = o_sb
+            dst = st[("o", b)][:, D * j : D * (j + 1)]
+            if engine == "s":
+                nc.scalar.activation(out=dst, in_=st[("s2", b, j)][:], func=ACT.Relu)
+            else:
+                nc.vector.tensor_scalar_max(out=dst, in0=st[("s2", b, j)][:], scalar1=0.0)
+
+        def store(b, lo, hi):
+            if not live(b):
+                return
+            part = slice(D * lo, D * hi)
+            nc.sync.dma_start(out=rows(out[b])[:, part], in_=st[("o", b)][:, part])
+
+        for b in range(NB):
             load(b)
-        for i in range(NB + 2):
-            if i + PRE < NB:
-                load(i + PRE)
-            if i < NB:
-                front(i)
-            if i == 0:
-                prepare_mask()
-            if 0 <= i - 1 < NB:
-                mid(i - 1)
-            if 0 <= i - 2 < NB:
-                back(i - 2)
+
+        transposes(0)
+        unpack("s", st[("qk", 0)][0][:].bitcast(F32), 0, st[("tp", 0)][0])
+        unpack("v", st[("qk", 0)][0][:].bitcast(F32), 1, st[("tp", 0)][1])
+        quantise_qk(0, 0)
+        unpack("s", st[("qk", 0)][0][:].bitcast(F32), 2, st[("tp", 0)][2])
+        unpack("v", st[("qk", 0)][0][:].bitcast(F32), 3, st[("tp", 0)][3])
+        quantise_qk(0, 1)
+        prepare_mask()
+        scores(0, 0)
+        scores(0, 1)
+        regroup(0, "v", 0, P)
+        transposes(1)
+        copies(1, "ssss")
+
+        last = NB - 1
+        for c in range(NB + 1):
+            logits(c, 0)
+            scores(c, 2)
+            logits(c, 1)
+            scores(c, 3)
+            if c - 1 == last:
+                result(last, 0, "s")
+                result(last, 1, "v")
+                store(last, 0, 2)
+                result(last, 2, "s")
+                result(last, 3, "v")
+                store(last, 2, 4)
+                break
+            result(c - 1, 0, "s")
+            product(c - 1, 2)
+            result(c - 1, 1, "s")
+            product(c - 1, 3)
+            logits(c, 2)
+            logits(c, 3)
+            split = 0 if c + 1 == last else R_VECTOR_GROUPS
+            regroup(c + 1, "s", split, P)
+            result(c - 1, 2, "s")
+            result(c - 1, 3, "s")
+            store(c - 1, 0, 4)
+            transposes(c + 2)
+            copies(c + 2, "ssss")
+            quantise_qk(c + 1, 0)
+            quantise_qk(c + 1, 1)
+            scores(c + 1, 0)
+            scores(c + 1, 1)
+            clamp(c)
+            quantise_v(c)
+            quantise_l(c)
+            product(c, 0)
+            product(c, 1)
+            if c == last:
+                product(c, 2, spare=True)
+                product(c, 3, spare=True)
+            regroup(c + 1, "v", 0, split)

@@ -19,8 +19,9 @@ P = 128
 FLOPS = 2 * 2 * NB * S * S * D
 
 INV_SQRT_D = 1.0 / math.sqrt(D)
-R_VECTOR_GROUPS = 56
+R_GPSIMD_GROUPS = 76
 MANUAL = True
+SCALAR_TAIL = 6
 
 
 def tile_scaledconvolutionaldotproduct_pa_t_kernel(tc, qp, kp, vp, mask, out):
@@ -31,8 +32,8 @@ def tile_scaledconvolutionaldotproduct_pa_t_kernel(tc, qp, kp, vp, mask, out):
         const = ctx.enter_context(tc.tile_pool(name="const", bufs=1))
         raw = ctx.enter_context(tc.tile_pool(name="raw", bufs=NB))
         work = ctx.enter_context(tc.tile_pool(name="work", bufs=2))
-        ps_t = ctx.enter_context(tc.psum_pool(name="ps_t", bufs=4))
-        ps_1 = ctx.enter_context(tc.psum_pool(name="ps_1", bufs=2))
+        ps_t = ctx.enter_context(tc.psum_pool(name="ps_t", bufs=3))
+        ps_1 = ctx.enter_context(tc.psum_pool(name="ps_1", bufs=3))
         ps_2 = ctx.enter_context(tc.psum_pool(name="ps_2", bufs=2))
 
         ident = const.tile([P, P], F32)
@@ -87,42 +88,36 @@ def tile_scaledconvolutionaldotproduct_pa_t_kernel(tc, qp, kp, vp, mask, out):
                         nc.tensor.transpose(tp[:, jj, u, :], m32[:, 2 * h + jj, :, u], ident[:])
                 unpack("s", g32, h, tp)
 
-        def transposes(b):
+        def transposes(b, n):
             if not live(b):
                 return
-            k_sb, q_sb, v_sb = st[("raw", b)]
-            banks = []
-            for src in (k_sb, q_sb):
-                s32 = src[:].bitcast(F32)
-                for h in range(2):
-                    tp = ps_t.tile([P, 2, 2, P], F32, tag="tp")
-                    for jj in range(2):
-                        for u in range(2):
-                            c0 = (2 * h + jj) * 256 + u * 128
-                            nc.tensor.transpose(tp[:, jj, u, :], s32[:, c0 : c0 + 128], ident[:])
-                    banks.append(tp)
-            st[("tp", b)] = banks
-            qk_g = work.tile([P, 8 * S], BF16, align_bytes=64)
-            qk_c = work.tile([P, 2 * S], U32, align_bytes=64)
-            qk_s = work.tile([P, 2 * S], U8, align_bytes=64)
-            st[("qk", b)] = (qk_g, qk_c, qk_s)
+            if n == 0:
+                qk_g = work.tile([P, 8 * S], BF16, align_bytes=64)
+                qk_c = work.tile([P, 2 * S], U32, align_bytes=64)
+                qk_s = work.tile([P, 2 * S], U8, align_bytes=64)
+                st[("qk", b)] = (qk_g, qk_c, qk_s)
+            s32 = st[("raw", b)][n // 2][:].bitcast(F32)
+            tp = ps_t.tile([P, 2, 2, P], F32, tag="tp")
+            for jj in range(2):
+                for u in range(2):
+                    c0 = (2 * (n % 2) + jj) * 256 + u * 128
+                    nc.tensor.transpose(tp[:, jj, u, :], s32[:, c0 : c0 + 128], ident[:])
+            st[("tp", b, n)] = tp
 
-        def copies(b, engines):
+        def copy(b, n, engine):
             if not live(b):
                 return
-            g32 = st[("qk", b)][0][:].bitcast(F32)
-            for n in range(4):
-                unpack(engines[n], g32, n, st[("tp", b)][n])
+            unpack(engine, st[("qk", b)][0][:].bitcast(F32), n, st[("tp", b, n)])
 
-        def quantise_qk(b, part):
+        def quantise_qk(b, lo, hi):
             if not live(b):
                 return
             qk_g, qk_c, qk_s = st[("qk", b)]
-            w = slice(S * part, S * (part + 1))
+            w = slice(S * lo, S * hi)
             nc.vector.quantize_mx(
                 out=qk_c[:, w].bitcast(FP8X4),
                 scales=qk_s[:, w],
-                in_=qk_g[:, 4 * S * part : 4 * S * (part + 1)],
+                in_=qk_g[:, 4 * S * lo : 4 * S * hi],
             )
 
         def scores(b, j):
@@ -147,11 +142,29 @@ def tile_scaledconvolutionaldotproduct_pa_t_kernel(tc, qp, kp, vp, mask, out):
         def logits(b, j):
             if not live(b):
                 return
+            cols = slice(4 * P * j, 4 * P * (j + 1))
+            if b >= SCALAR_TAIL:
+                if j == 0:
+                    l_g = work.tile([P, 4 * S], BF16, align_bytes=64)
+                    st[("l", b)] = l_g
+                a = work.tile([P, P, 4], F32, bufs=3)
+                nc.scalar.activation(
+                    out=a[:],
+                    in_=st[("s1", b, j)][:].rearrange("p t r -> p r t"),
+                    func=ACT.Relu,
+                    scale=INV_SQRT_D,
+                )
+                nc.vector.tensor_tensor(
+                    out=st[("l", b)][:, cols],
+                    in0=a[:].rearrange("p r t -> p (r t)"),
+                    in1=mask_g[:, cols],
+                    op=ALU.add,
+                )
+                return
             if j == 0:
                 x_g = work.tile([P, 4 * S], BF16, align_bytes=64)
                 st[("x", b)] = x_g
             x_g = st[("x", b)]
-            cols = slice(4 * P * j, 4 * P * (j + 1))
             nc.vector.scalar_tensor_tensor(
                 out=x_g[:, cols].rearrange("p (r t) -> p r t", t=4),
                 in0=st[("s1", b, j)][:].rearrange("p t r -> p r t"),
@@ -162,19 +175,26 @@ def tile_scaledconvolutionaldotproduct_pa_t_kernel(tc, qp, kp, vp, mask, out):
             )
 
         def clamp(b):
-            if not live(b):
+            if not live(b) or b >= SCALAR_TAIL:
                 return
             l_g = work.tile([P, 4 * S], BF16, align_bytes=64)
             nc.vector.tensor_tensor(out=l_g[:], in0=st[("x", b)][:], in1=mask_g[:], op=ALU.max)
             st[("l", b)] = l_g
 
-        def quantise_l(b):
+        def quantise_l(b, lo, hi):
             if not live(b):
                 return
-            l_c = work.tile([P, S], U32, align_bytes=64)
-            l_s = work.tile([P, S], U8, align_bytes=64)
-            nc.vector.quantize_mx(out=l_c[:].bitcast(FP8X4), scales=l_s[:], in_=st[("l", b)][:])
-            st[("lc", b)] = (l_c, l_s)
+            if lo == 0:
+                l_c = work.tile([P, S], U32, align_bytes=64)
+                l_s = work.tile([P, S], U8, align_bytes=64)
+                st[("lc", b)] = (l_c, l_s)
+            l_c, l_s = st[("lc", b)]
+            w = slice(P * lo, P * hi)
+            nc.vector.quantize_mx(
+                out=l_c[:, w].bitcast(FP8X4),
+                scales=l_s[:, w],
+                in_=st[("l", b)][:, 4 * P * lo : 4 * P * hi],
+            )
 
         def regroup(b, engine, lo, hi):
             if not live(b) or lo == hi:
@@ -182,11 +202,14 @@ def tile_scaledconvolutionaldotproduct_pa_t_kernel(tc, qp, kp, vp, mask, out):
             if ("vg", b) not in st:
                 v_g = work.tile([P, 4 * D], BF16, align_bytes=64)
                 st[("vg", b)] = v_g
-            copy_out(
-                engine,
-                st[("vg", b)][:].rearrange("p (c i t) -> p c t i", i=4, t=4)[:, lo:hi],
-                st[("raw", b)][2][:].rearrange("p (t c i) -> p c t i", i=4, t=4)[:, lo:hi],
-            )
+            dst = st[("vg", b)][:].rearrange("p (c i t) -> p c t i", i=4, t=4)[:, lo:hi]
+            src = st[("raw", b)][2][:].rearrange("p (t c i) -> p c t i", i=4, t=4)[:, lo:hi]
+            if engine == "g":
+                nc.gpsimd.tensor_scalar(
+                    out=dst, in0=src, scalar1=1.0, scalar2=0.0, op0=ALU.mult, op1=ALU.add
+                )
+            else:
+                copy_out(engine, dst, src)
 
         def quantise_v(b):
             if not live(b):
@@ -238,57 +261,73 @@ def tile_scaledconvolutionaldotproduct_pa_t_kernel(tc, qp, kp, vp, mask, out):
         for b in range(NB):
             load(b)
 
-        transposes(0)
-        unpack("s", st[("qk", 0)][0][:].bitcast(F32), 0, st[("tp", 0)][0])
-        unpack("v", st[("qk", 0)][0][:].bitcast(F32), 1, st[("tp", 0)][1])
-        quantise_qk(0, 0)
-        unpack("s", st[("qk", 0)][0][:].bitcast(F32), 2, st[("tp", 0)][2])
-        unpack("v", st[("qk", 0)][0][:].bitcast(F32), 3, st[("tp", 0)][3])
-        quantise_qk(0, 1)
+        for n in range(3):
+            transposes(0, n)
+        copy(0, 0, "s")
+        transposes(0, 3)
+        copy(0, 1, "v")
+        quantise_qk(0, 0, 1)
+        copy(0, 2, "s")
+        copy(0, 3, "v")
+        quantise_qk(0, 1, 2)
         prepare_mask()
-        scores(0, 0)
-        scores(0, 1)
+        for j in range(3):
+            scores(0, j)
         regroup(0, "v", 0, P)
-        transposes(1)
-        copies(1, "ssss")
+        for n in range(3):
+            transposes(1, n)
+        copy(1, 0, "s")
+        transposes(1, 3)
+        for n in range(1, 4):
+            copy(1, n, "s")
 
         last = NB - 1
-        for c in range(NB + 1):
+        for c in range(NB):
+            split = 0 if c + 1 == last else R_GPSIMD_GROUPS
+            regroup(c + 1, "g", 0, split // 2)
+            regroup(c + 1, "g", split // 2, split)
             logits(c, 0)
-            scores(c, 2)
-            logits(c, 1)
             scores(c, 3)
-            if c - 1 == last:
-                result(last, 0, "s")
-                result(last, 1, "v")
-                store(last, 0, 2)
-                result(last, 2, "s")
-                result(last, 3, "v")
-                store(last, 2, 4)
-                break
+            logits(c, 1)
+            if c == last:
+                quantise_l(c, 0, 2)
+                product(c, 0, spare=True)
+                product(c, 1, spare=True)
             result(c - 1, 0, "s")
             product(c - 1, 2)
             result(c - 1, 1, "s")
             product(c - 1, 3)
             logits(c, 2)
             logits(c, 3)
-            split = 0 if c + 1 == last else R_VECTOR_GROUPS
             regroup(c + 1, "s", split, P)
             result(c - 1, 2, "s")
             result(c - 1, 3, "s")
             store(c - 1, 0, 4)
-            transposes(c + 2)
-            copies(c + 2, "ssss")
-            quantise_qk(c + 1, 0)
-            quantise_qk(c + 1, 1)
-            scores(c + 1, 0)
-            scores(c + 1, 1)
+            if c == last:
+                quantise_l(c, 2, 4)
+                product(c, 2)
+                product(c, 3)
+                result(c, 0, "s")
+                result(c, 1, "v")
+                store(c, 0, 2)
+                result(c, 2, "s")
+                store(c, 2, 3)
+                result(c, 3, "v")
+                store(c, 3, 4)
+                break
+            for n in range(3):
+                transposes(c + 2, n)
+            copy(c + 2, 0, "s")
+            transposes(c + 2, 3)
+            for n in range(1, 4):
+                copy(c + 2, n, "s")
             clamp(c)
+            quantise_qk(c + 1, 0, 2)
+            for j in range(3):
+                scores(c + 1, j)
+            quantise_l(c, 0, 4)
             quantise_v(c)
-            quantise_l(c)
+            if c + 1 == last:
+                quantise_v(last)
             product(c, 0)
             product(c, 1)
-            if c == last:
-                product(c, 2, spare=True)
-                product(c, 3, spare=True)
-            regroup(c + 1, "v", 0, split)

@@ -93,9 +93,7 @@ def tile_scaledconvolutionaldotproduct_pa_t_kernel(tc, qp, kp, vp, mask, out):
                 return
             if n == 0:
                 qk_g = work.tile([P, 8 * S], BF16, align_bytes=64)
-                qk_c = work.tile([P, 2 * S], U32, align_bytes=64)
-                qk_s = work.tile([P, 2 * S], U8, align_bytes=64)
-                st[("qk", b)] = (qk_g, qk_c, qk_s)
+                st[("qkg", b)] = qk_g
             s32 = st[("raw", b)][n // 2][:].bitcast(F32)
             tp = ps_t.tile([P, 2, 2, P], F32, tag="tp")
             for jj in range(2):
@@ -107,12 +105,17 @@ def tile_scaledconvolutionaldotproduct_pa_t_kernel(tc, qp, kp, vp, mask, out):
         def copy(b, n, engine):
             if not live(b):
                 return
-            unpack(engine, st[("qk", b)][0][:].bitcast(F32), n, st[("tp", b, n)])
+            unpack(engine, st[("qkg", b)][:].bitcast(F32), n, st[("tp", b, n)])
 
         def quantise_qk(b, lo, hi):
             if not live(b):
                 return
-            qk_g, qk_c, qk_s = st[("qk", b)]
+            if lo == 0:
+                qk_c = work.tile([P, 2 * S], U32, align_bytes=64)
+                qk_s = work.tile([P, 2 * S], U8, align_bytes=64)
+                st[("qk", b)] = (qk_c, qk_s)
+            qk_g = st[("qkg", b)]
+            qk_c, qk_s = st[("qk", b)]
             w = slice(S * lo, S * hi)
             nc.vector.quantize_mx(
                 out=qk_c[:, w].bitcast(FP8X4),
@@ -123,8 +126,11 @@ def tile_scaledconvolutionaldotproduct_pa_t_kernel(tc, qp, kp, vp, mask, out):
         def scores(b, j):
             if not live(b):
                 return
-            qk_g, qk_c, qk_s = st[("qk", b)]
-            s1 = ps_1.tile([P, 4, P], F32, tag="s1")
+            qk_c, qk_s = st[("qk", b)]
+            if ("s1", b, j) not in st:
+                s1 = ps_1.tile([P, 4, P], F32, tag="s1")
+                st[("s1", b, j)] = s1
+            s1 = st[("s1", b, j)]
             for t in range(4):
                 kc = slice(P * t, P * (t + 1))
                 qc = slice(S + P * j, S + P * (j + 1))
@@ -137,7 +143,24 @@ def tile_scaledconvolutionaldotproduct_pa_t_kernel(tc, qp, kp, vp, mask, out):
                     start=True,
                     stop=True,
                 )
-            st[("s1", b, j)] = s1
+
+        def idle_passes(b, src, count):
+            if not live(b):
+                return
+            qk_c, qk_s = st[("qk", src)]
+            if ("s1", b, 0) not in st:
+                s1 = ps_1.tile([P, 4, P], F32, tag="s1")
+                st[("s1", b, 0)] = s1
+            for i in range(count):
+                nc.tensor.matmul_mx(
+                    out=st[("s1", b, 0)][:].rearrange("p t r -> p (t r)"),
+                    lhsT=qk_c[:, 0:P].bitcast(FP8X4),
+                    lhsT_scale=qk_s[:, 0:P],
+                    rhs=qk_c[:, 0:S].bitcast(FP8X4),
+                    rhs_scale=qk_s[:, 0:S],
+                    start=True,
+                    stop=True,
+                )
 
         def logits(b, j):
             if not live(b):
@@ -271,6 +294,7 @@ def tile_scaledconvolutionaldotproduct_pa_t_kernel(tc, qp, kp, vp, mask, out):
         copy(0, 3, "v")
         quantise_qk(0, 1, 2)
         prepare_mask()
+        idle_passes(0, 0, 3)
         for j in range(3):
             scores(0, j)
         regroup(0, "v", 0, P)
@@ -300,6 +324,12 @@ def tile_scaledconvolutionaldotproduct_pa_t_kernel(tc, qp, kp, vp, mask, out):
             logits(c, 2)
             logits(c, 3)
             regroup(c + 1, "s", split, P)
+            if c != last:
+                idle_passes(c + 1, c, 2)
+                for n in range(3):
+                    transposes(c + 2, n)
+                copy(c + 2, 0, "s")
+                transposes(c + 2, 3)
             result(c - 1, 2, "s")
             result(c - 1, 3, "s")
             store(c - 1, 0, 4)
@@ -315,12 +345,9 @@ def tile_scaledconvolutionaldotproduct_pa_t_kernel(tc, qp, kp, vp, mask, out):
                 result(c, 3, "v")
                 store(c, 3, 4)
                 break
-            for n in range(3):
-                transposes(c + 2, n)
-            copy(c + 2, 0, "s")
-            transposes(c + 2, 3)
             for n in range(1, 4):
                 copy(c + 2, n, "s")
+            idle_passes(c + 1, c, 3)
             clamp(c)
             quantise_qk(c + 1, 0, 2)
             for j in range(3):

@@ -19,7 +19,7 @@ P = 128
 FLOPS = 2 * 2 * NB * S * S * D
 
 INV_SQRT_D = 1.0 / math.sqrt(D)
-R_GPSIMD_GROUPS = 76
+R_GPSIMD_GROUPS = 48
 MANUAL = True
 SCALAR_TAIL = 6
 
@@ -54,11 +54,16 @@ def tile_scaledconvolutionaldotproduct_pa_t_kernel(tc, qp, kp, vp, mask, out):
             q_sb = raw.tile([P, 4 * D], BF16)
             v_sb = raw.tile([P, 4 * D], BF16)
             if b == 0:
-                for x_sb, x in ((k_sb, kp), (q_sb, qp)):
-                    for h in range(2):
-                        half = slice(2 * D * h, 2 * D * (h + 1))
-                        nc.sync.dma_start(out=x_sb[:, half], in_=rows(x[b])[:, half])
-                nc.sync.dma_start(out=m_sb[:], in_=rows(mask[0]))
+                for x_sb, x, h in (
+                    (k_sb, kp[0], 0),
+                    (k_sb, kp[0], 1),
+                    (q_sb, qp[0], 0),
+                    (m_sb, mask[0], 0),
+                    (q_sb, qp[0], 1),
+                    (m_sb, mask[0], 1),
+                ):
+                    half = slice(2 * D * h, 2 * D * (h + 1))
+                    nc.sync.dma_start(out=x_sb[:, half], in_=rows(x)[:, half])
             else:
                 nc.sync.dma_start(out=k_sb[:], in_=rows(kp[b]))
                 nc.sync.dma_start(out=q_sb[:], in_=rows(qp[b]))
@@ -78,15 +83,16 @@ def tile_scaledconvolutionaldotproduct_pa_t_kernel(tc, qp, kp, vp, mask, out):
                 tp[:].rearrange("p j u r -> p j r u"),
             )
 
-        def prepare_mask():
+        def mask_transposes(h):
             m32 = m_sb[:].bitcast(F32).rearrange("r (j p u) -> r j p u", j=4, u=2)
-            g32 = mask_g[:].bitcast(F32)
-            for h in range(2):
-                tp = ps_2.tile([P, 2, 2, P], F32, tag="s2")
-                for jj in range(2):
-                    for u in range(2):
-                        nc.tensor.transpose(tp[:, jj, u, :], m32[:, 2 * h + jj, :, u], ident[:])
-                unpack("s", g32, h, tp)
+            tp = ps_2.tile([P, 2, 2, P], F32, tag="s2")
+            for jj in range(2):
+                for u in range(2):
+                    nc.tensor.transpose(tp[:, jj, u, :], m32[:, 2 * h + jj, :, u], ident[:])
+            st[("mt", h)] = tp
+
+        def mask_copy(h):
+            unpack("s", mask_g[:].bitcast(F32), h, st[("mt", h)])
 
         def transposes(b, n):
             if not live(b):
@@ -116,11 +122,11 @@ def tile_scaledconvolutionaldotproduct_pa_t_kernel(tc, qp, kp, vp, mask, out):
                 st[("qk", b)] = (qk_c, qk_s)
             qk_g = st[("qkg", b)]
             qk_c, qk_s = st[("qk", b)]
-            w = slice(S * lo, S * hi)
+            w = slice(2 * P * lo, 2 * P * hi)
             nc.vector.quantize_mx(
                 out=qk_c[:, w].bitcast(FP8X4),
                 scales=qk_s[:, w],
-                in_=qk_g[:, 4 * S * lo : 4 * S * hi],
+                in_=qk_g[:, 8 * P * lo : 8 * P * hi],
             )
 
         def scores(b, j):
@@ -140,24 +146,6 @@ def tile_scaledconvolutionaldotproduct_pa_t_kernel(tc, qp, kp, vp, mask, out):
                     lhsT_scale=qk_s[:, kc],
                     rhs=qk_c[:, qc].bitcast(FP8X4),
                     rhs_scale=qk_s[:, qc],
-                    start=True,
-                    stop=True,
-                )
-
-        def idle_passes(b, src, count):
-            if not live(b):
-                return
-            qk_c, qk_s = st[("qk", src)]
-            if ("s1", b, 0) not in st:
-                s1 = ps_1.tile([P, 4, P], F32, tag="s1")
-                st[("s1", b, 0)] = s1
-            for i in range(count):
-                nc.tensor.matmul_mx(
-                    out=st[("s1", b, 0)][:].rearrange("p t r -> p (t r)"),
-                    lhsT=qk_c[:, 0:P].bitcast(FP8X4),
-                    lhsT_scale=qk_s[:, 0:P],
-                    rhs=qk_c[:, 0:S].bitcast(FP8X4),
-                    rhs_scale=qk_s[:, 0:S],
                     start=True,
                     stop=True,
                 )
@@ -287,32 +275,38 @@ def tile_scaledconvolutionaldotproduct_pa_t_kernel(tc, qp, kp, vp, mask, out):
         for n in range(3):
             transposes(0, n)
         copy(0, 0, "s")
-        transposes(0, 3)
         copy(0, 1, "v")
-        quantise_qk(0, 0, 1)
+        mask_transposes(0)
+        quantise_qk(0, 0, 2)
         copy(0, 2, "s")
-        copy(0, 3, "v")
-        quantise_qk(0, 1, 2)
-        prepare_mask()
-        idle_passes(0, 0, 3)
-        for j in range(3):
-            scores(0, j)
-        regroup(0, "v", 0, P)
-        for n in range(3):
-            transposes(1, n)
-        copy(1, 0, "s")
-        transposes(1, 3)
-        for n in range(1, 4):
-            copy(1, n, "s")
+        transposes(0, 3)
+        mask_copy(0)
+        quantise_qk(0, 2, 3)
+        scores(0, 0)
+        scores(0, 1)
+        mask_transposes(1)
+        copy(0, 3, "s")
+        mask_copy(1)
+        regroup(0, "g", 0, P // 2)
+        regroup(0, "g", P // 2, P)
 
         last = NB - 1
         for c in range(NB):
             split = 0 if c + 1 == last else R_GPSIMD_GROUPS
-            regroup(c + 1, "g", 0, split // 2)
-            regroup(c + 1, "g", split // 2, split)
+            regroup(c + 1, "g", 0, split)
             logits(c, 0)
+            if c == 0:
+                quantise_qk(0, 3, 4)
+                scores(0, 2)
             scores(c, 3)
             logits(c, 1)
+            if c == 0:
+                for n in range(3):
+                    transposes(1, n)
+                copy(1, 0, "s")
+                transposes(1, 3)
+                for n in range(1, 4):
+                    copy(1, n, "s")
             if c == last:
                 quantise_l(c, 0, 2)
                 product(c, 0, spare=True)
@@ -325,7 +319,6 @@ def tile_scaledconvolutionaldotproduct_pa_t_kernel(tc, qp, kp, vp, mask, out):
             logits(c, 3)
             regroup(c + 1, "s", split, P)
             if c != last:
-                idle_passes(c + 1, c, 2)
                 for n in range(3):
                     transposes(c + 2, n)
                 copy(c + 2, 0, "s")
@@ -347,9 +340,8 @@ def tile_scaledconvolutionaldotproduct_pa_t_kernel(tc, qp, kp, vp, mask, out):
                 break
             for n in range(1, 4):
                 copy(c + 2, n, "s")
-            idle_passes(c + 1, c, 3)
             clamp(c)
-            quantise_qk(c + 1, 0, 2)
+            quantise_qk(c + 1, 0, 4)
             for j in range(3):
                 scores(c + 1, j)
             quantise_l(c, 0, 4)

@@ -255,7 +255,7 @@ def tile_scaledconvolutionaldotproduct_pa_t_kernel(tc, qp, kp, vp, mask, out):
             if not live(b):
                 return
             if j == 0:
-                o_sb = work.tile([P, 4 * D], F32, bufs=3)
+                o_sb = work.tile([P, 4 * D], F32, bufs=5)
                 st[("o", b)] = o_sb
             dst = st[("o", b)][:, D * j : D * (j + 1)]
             if engine == "s":

import math
from contextlib import ExitStack

import concourse.mybir as mybir
from concourse.masks import make_identity

F32 = mybir.dt.float32
BF16 = mybir.dt.bfloat16
U32 = mybir.dt.uint32
U8 = mybir.dt.uint8
FP8X4 = mybir.dt.float8_e4m3fn_x4
ALU = mybir.AluOpType
ACT = mybir.ActivationFunctionType

NB = 8
S = 512
D = 512
P = 128
FLOPS = 2 * 2 * NB * S * S * D

INV_SQRT_D = 1.0 / math.sqrt(D)
R_GPSIMD_GROUPS = 48
MANUAL = True
SCALAR_TAIL = 6


def tile_scaledconvolutionaldotproduct_pa_t_kernel(tc, qp, kp, vp, mask, out):
    nc = tc.nc
    with ExitStack() as ctx:
        if MANUAL:
            ctx.enter_context(tc.manual_schedule())
        const = ctx.enter_context(tc.tile_pool(name="const", bufs=1))
        raw = ctx.enter_context(tc.tile_pool(name="raw", bufs=NB))
        work = ctx.enter_context(tc.tile_pool(name="work", bufs=2))
        ps_t = ctx.enter_context(tc.psum_pool(name="ps_t", bufs=3))
        ps_1 = ctx.enter_context(tc.psum_pool(name="ps_1", bufs=3))
        ps_2 = ctx.enter_context(tc.psum_pool(name="ps_2", bufs=2))

        ident = const.tile([P, P], F32)
        make_identity(nc, ident[:])
        m_sb = const.tile([P, 4 * S], BF16)
        mask_g = const.tile([P, 4 * S], BF16, align_bytes=64)

        st = {}

        def live(b):
            return 0 <= b < NB

        def rows(x):
            return x.rearrange("(p j) d -> p (j d)", j=4)

        def load(b):
            k_sb = raw.tile([P, 4 * D], BF16)
            q_sb = raw.tile([P, 4 * D], BF16)
            v_sb = raw.tile([P, 4 * D], BF16)
            if b == 0:
                for x_sb, x, h in (
                    (k_sb, kp[0], 0),
                    (k_sb, kp[0], 1),
                    (q_sb, qp[0], 0),
                    (m_sb, mask[0], 0),
                    (q_sb, qp[0], 1),
                    (m_sb, mask[0], 1),
                ):
                    half = slice(2 * D * h, 2 * D * (h + 1))
                    nc.sync.dma_start(out=x_sb[:, half], in_=rows(x)[:, half])
            else:
                nc.sync.dma_start(out=k_sb[:], in_=rows(kp[b]))
                nc.sync.dma_start(out=q_sb[:], in_=rows(qp[b]))
            nc.sync.dma_start(out=v_sb[:], in_=rows(vp[b]))
            st[("raw", b)] = (k_sb, q_sb, v_sb)

        def copy_out(engine, dst, src):
            if engine == "s":
                nc.scalar.copy(out=dst, in_=src)
            else:
                nc.vector.tensor_copy(out=dst, in_=src)

        def unpack(engine, g32, n, tp):
            copy_out(
                engine,
                g32[:, 512 * n : 512 * (n + 1)].rearrange("p (j r u) -> p j r u", j=2, u=2),
                tp[:].rearrange("p j u r -> p j r u"),
            )

        def mask_transposes(h):
            m32 = m_sb[:].bitcast(F32).rearrange("r (j p u) -> r j p u", j=4, u=2)
            tp = ps_2.tile([P, 2, 2, P], F32, tag="s2")
            for jj in range(2):
                for u in range(2):
                    nc.tensor.transpose(tp[:, jj, u, :], m32[:, 2 * h + jj, :, u], ident[:])
            st[("mt", h)] = tp

        def mask_copy(h):
            unpack("s", mask_g[:].bitcast(F32), h, st[("mt", h)])

        def transposes(b, n):
            if not live(b):
                return
            if n == 0:
                qk_g = work.tile([P, 8 * S], BF16, align_bytes=64)
                st[("qkg", b)] = qk_g
            s32 = st[("raw", b)][n // 2][:].bitcast(F32)
            tp = ps_t.tile([P, 2, 2, P], F32, tag="tp")
            for jj in range(2):
                for u in range(2):
                    c0 = (2 * (n % 2) + jj) * 256 + u * 128
                    nc.tensor.transpose(tp[:, jj, u, :], s32[:, c0 : c0 + 128], ident[:])
            st[("tp", b, n)] = tp

        def copy(b, n, engine):
            if not live(b):
                return
            unpack(engine, st[("qkg", b)][:].bitcast(F32), n, st[("tp", b, n)])

        def quantise_qk(b, lo, hi):
            if not live(b):
                return
            if lo == 0:
                qk_c = work.tile([P, 2 * S], U32, align_bytes=64)
                qk_s = work.tile([P, 2 * S], U8, align_bytes=64)
                st[("qk", b)] = (qk_c, qk_s)
            qk_g = st[("qkg", b)]
            qk_c, qk_s = st[("qk", b)]
            w = slice(2 * P * lo, 2 * P * hi)
            nc.vector.quantize_mx(
                out=qk_c[:, w].bitcast(FP8X4),
                scales=qk_s[:, w],
                in_=qk_g[:, 8 * P * lo : 8 * P * hi],
            )

        def scores(b, j):
            if not live(b):
                return
            qk_c, qk_s = st[("qk", b)]
            if ("s1", b, j) not in st:
                s1 = ps_1.tile([P, 4, P], F32, tag="s1")
                st[("s1", b, j)] = s1
            s1 = st[("s1", b, j)]
            for t in range(4):
                kc = slice(P * t, P * (t + 1))
                qc = slice(S + P * j, S + P * (j + 1))
                nc.tensor.matmul_mx(
                    out=s1[:, t, :],
                    lhsT=qk_c[:, kc].bitcast(FP8X4),
                    lhsT_scale=qk_s[:, kc],
                    rhs=qk_c[:, qc].bitcast(FP8X4),
                    rhs_scale=qk_s[:, qc],
                    start=True,
                    stop=True,
                )

        def logits(b, j):
            if not live(b):
                return
            cols = slice(4 * P * j, 4 * P * (j + 1))
            if b >= SCALAR_TAIL:
                if j == 0:
                    l_g = work.tile([P, 4 * S], BF16, align_bytes=64)
                    st[("l", b)] = l_g
                a = work.tile([P, P, 4], F32, bufs=3)
                nc.scalar.activation(
                    out=a[:],
                    in_=st[("s1", b, j)][:].rearrange("p t r -> p r t"),
                    func=ACT.Relu,
                    scale=INV_SQRT_D,
                )
                nc.vector.tensor_tensor(
                    out=st[("l", b)][:, cols],
                    in0=a[:].rearrange("p r t -> p (r t)"),
                    in1=mask_g[:, cols],
                    op=ALU.add,
                )
                return
            if j == 0:
                x_g = work.tile([P, 4 * S], BF16, align_bytes=64)
                st[("x", b)] = x_g
            x_g = st[("x", b)]
            nc.vector.scalar_tensor_tensor(
                out=x_g[:, cols].rearrange("p (r t) -> p r t", t=4),
                in0=st[("s1", b, j)][:].rearrange("p t r -> p r t"),
                scalar=INV_SQRT_D,
                in1=mask_g[:, cols].rearrange("p (r t) -> p r t", t=4),
                op0=ALU.mult,
                op1=ALU.add,
            )

        def clamp(b):
            if not live(b) or b >= SCALAR_TAIL:
                return
            l_g = work.tile([P, 4 * S], BF16, align_bytes=64)
            nc.vector.tensor_tensor(out=l_g[:], in0=st[("x", b)][:], in1=mask_g[:], op=ALU.max)
            st[("l", b)] = l_g

        def quantise_l(b, lo, hi):
            if not live(b):
                return
            if lo == 0:
                l_c = work.tile([P, S], U32, align_bytes=64)
                l_s = work.tile([P, S], U8, align_bytes=64)
                st[("lc", b)] = (l_c, l_s)
            l_c, l_s = st[("lc", b)]
            w = slice(P * lo, P * hi)
            nc.vector.quantize_mx(
                out=l_c[:, w].bitcast(FP8X4),
                scales=l_s[:, w],
                in_=st[("l", b)][:, 4 * P * lo : 4 * P * hi],
            )

        def regroup(b, engine, lo, hi):
            if not live(b) or lo == hi:
                return
            if ("vg", b) not in st:
                v_g = work.tile([P, 4 * D], BF16, align_bytes=64)
                st[("vg", b)] = v_g
            dst = st[("vg", b)][:].rearrange("p (c i t) -> p c t i", i=4, t=4)[:, lo:hi]
            src = st[("raw", b)][2][:].rearrange("p (t c i) -> p c t i", i=4, t=4)[:, lo:hi]
            if engine == "g":
                nc.gpsimd.tensor_scalar(
                    out=dst, in0=src, scalar1=1.0, scalar2=0.0, op0=ALU.mult, op1=ALU.add
                )
            else:
                copy_out(engine, dst, src)

        def quantise_v(b):
            if not live(b):
                return
            v_c = work.tile([P, D], U32, align_bytes=64)
            v_s = work.tile([P, D], U8, align_bytes=64)
            nc.vector.quantize_mx(out=v_c[:].bitcast(FP8X4), scales=v_s[:], in_=st[("vg", b)][:])
            st[("vc", b)] = (v_c, v_s)

        def product(b, j, spare=False):
            if not live(b):
                return
            l_c, l_s = st[("lc", b)]
            v_c, v_s = st[("vc", b)]
            if spare:
                s2 = ps_t.tile([P, D], F32, tag="tp")
            else:
                s2 = ps_2.tile([P, D], F32, tag="s2")
            qc = slice(P * j, P * (j + 1))
            nc.tensor.matmul_mx(
                out=s2[:],
                lhsT=l_c[:, qc].bitcast(FP8X4),
                lhsT_scale=l_s[:, qc],
                rhs=v_c[:].bitcast(FP8X4),
                rhs_scale=v_s[:],
                start=True,
                stop=True,
            )
            st[("s2", b, j)] = s2

        def result(b, j, engine):
            if not live(b):
                return
            if j == 0:
                o_sb = work.tile([P, 4 * D], F32, bufs=5)
                st[("o", b)] = o_sb
            dst = st[("o", b)][:, D * j : D * (j + 1)]
            if engine == "s":
                nc.scalar.activation(out=dst, in_=st[("s2", b, j)][:], func=ACT.Relu)
            else:
                nc.vector.tensor_scalar_max(out=dst, in0=st[("s2", b, j)][:], scalar1=0.0)

        def store(b, lo, hi):
            if not live(b):
                return
            part = slice(D * lo, D * hi)
            nc.sync.dma_start(out=rows(out[b])[:, part], in_=st[("o", b)][:, part])

        for b in range(NB):
            load(b)

        for n in range(3):
            transposes(0, n)
        copy(0, 0, "s")
        copy(0, 1, "v")
        mask_transposes(0)
        quantise_qk(0, 0, 2)
        copy(0, 2, "s")
        transposes(0, 3)
        mask_copy(0)
        quantise_qk(0, 2, 3)
        scores(0, 0)
        scores(0, 1)
        mask_transposes(1)
        copy(0, 3, "s")
        mask_copy(1)
        regroup(0, "g", 0, P // 2)
        regroup(0, "g", P // 2, P)

        last = NB - 1
        for c in range(NB):
            split = 0 if c + 1 == last else R_GPSIMD_GROUPS
            regroup(c + 1, "g", 0, split)
            logits(c, 0)
            if c == 0:
                quantise_qk(0, 3, 4)
                scores(0, 2)
            scores(c, 3)
            logits(c, 1)
            if c == 0:
                for n in range(3):
                    transposes(1, n)
                copy(1, 0, "s")
                transposes(1, 3)
                for n in range(1, 4):
                    copy(1, n, "s")
            if c == last:
                quantise_l(c, 0, 2)
                product(c, 0, spare=True)
                product(c, 1, spare=True)
            result(c - 1, 0, "s")
            product(c - 1, 2)
            result(c - 1, 1, "s")
            product(c - 1, 3)
            logits(c, 2)
            logits(c, 3)
            regroup(c + 1, "s", split, P)
            if c != last:
                for n in range(3):
                    transposes(c + 2, n)
                copy(c + 2, 0, "s")
                transposes(c + 2, 3)
            result(c - 1, 2, "s")
            result(c - 1, 3, "s")
            store(c - 1, 0, 4)
            if c == last:
                quantise_l(c, 2, 4)
                product(c, 2)
                product(c, 3)
                result(c, 0, "s")
                result(c, 1, "v")
                store(c, 0, 2)
                result(c, 2, "s")
                store(c, 2, 3)
                result(c, 3, "v")
                store(c, 3, 4)
                break
            for n in range(1, 4):
                copy(c + 2, n, "s")
            clamp(c)
            quantise_qk(c + 1, 0, 4)
            for j in range(3):
                scores(c + 1, j)
            quantise_l(c, 0, 4)
            quantise_v(c)
            if c + 1 == last:
                quantise_v(last)
            product(c, 0)
            product(c, 1)
